import numpy as np
import ml_dtypes


def mxq(x, axis, fmt="e4m3"):
    dtype, down = {"e4m3": (ml_dtypes.float8_e4m3fn, 7), "e5m2": (ml_dtypes.float8_e5m2, 14)}[fmt]
    v = np.moveaxis(np.asarray(x, np.float32).astype(ml_dtypes.bfloat16).astype(np.float64), axis, -1)
    blocks = v.reshape(v.shape[:-1] + (-1, 32))
    amax = np.abs(blocks).max(-1, keepdims=True)
    byte = np.maximum(np.where(amax > 0, np.frexp(amax)[1] - 1 + 127, 0) - down, 1)
    scale = np.exp2(byte - 127.0)
    codes = (blocks / scale).astype(np.float32).astype(dtype).astype(np.float64)
    return np.moveaxis((codes * scale).reshape(v.shape), -1, axis)


WIDE = False


def mx_kscale(k):
    if not WIDE:
        return np.ones(k)
    levels = np.array([10, -10, 5, -5, 0])
    a = np.random.permutation(np.resize(levels, k // 512 * 4)).reshape(k // 512, 4)
    idx = np.arange(k)
    return np.exp2(a[idx // 512, idx % 128 // 32])


BF16 = ml_dtypes.bfloat16


def bf(x):
    return np.asarray(x, np.float32).astype(BF16)


def f64(x):
    return np.asarray(x).astype(np.float64)


E2M1 = np.array([0.0, 0.5, 1.0, 1.5, 2.0, 3.0, 4.0, 6.0, -0.0, -0.5, -1.0, -1.5, -2.0, -3.0, -4.0, -6.0])


def pack_weight(w, fmt):
    k, n = w.shape
    w = f64(bf(w)).reshape(k // 32, 32, n)
    amax = np.abs(w).max(1)
    if fmt == "e4m3":
        byte = np.frexp(amax)[1] - 1 + 127 - 7
    else:
        mant, ex = np.frexp(amax / 6.0)
        byte = np.where(mant > 0.5, ex, ex - 1) + 127
    byte = np.clip(np.where(amax > 0, byte, 1), 1, 254)
    scaled = (w * np.exp2(127.0 - byte)[:, None, :]).reshape(k, n).astype(np.float32)
    by_word = np.ascontiguousarray(scaled.reshape(k // 512, 128, 4, n).transpose(0, 1, 3, 2))
    if fmt == "e4m3":
        words = by_word.astype(ml_dtypes.float8_e4m3fn).view(np.uint8)
    else:
        c = by_word.astype(ml_dtypes.float4_e2m1fn).view(np.uint8) & 0xF
        words = c[..., 0::2] | (c[..., 1::2] << 4)
    return np.ascontiguousarray(words), np.ascontiguousarray(byte.astype(np.uint8).reshape(k // 512, 16, n))


def unpack_weight(words, scales, fmt):
    g, p, n, _ = words.shape
    if fmt == "e4m3":
        vals = np.ascontiguousarray(words).view(ml_dtypes.float8_e4m3fn).astype(np.float64)
    else:
        nib = np.empty((g, p, n, 4), np.uint8)
        nib[..., 0::2] = words & 0xF
        nib[..., 1::2] = words >> 4
        vals = E2M1[nib]
    vals = vals * np.repeat(np.exp2(scales.astype(np.float64) - 127.0), 8, axis=1)[..., None]
    return vals.transpose(0, 1, 3, 2).reshape(g * 512, n)


B, IN, HID = 4096, 512, 512
FMT = "e4m3"


def sigmoid(v):
    return 1.0 / (1.0 + np.exp(-v))


def lin(xq, words, scales):
    return xq @ unpack_weight(words, scales, FMT)


def setup_inputs():
    s, p = mx_kscale(IN), mx_kscale(HID)
    inputs = bf(np.random.standard_normal((B, IN)) * s)
    state = bf(np.random.standard_normal((B, HID)))
    parent_state = bf(np.random.standard_normal((B, HID)) * p)
    c = bf(np.tanh(np.random.standard_normal((B, HID))))
    w_a_w_words, w_a_w_scales = pack_weight((np.random.standard_normal((HID, IN)) * 0.6 / np.sqrt(IN) / s).T, FMT)
    w_a_b = bf(np.random.standard_normal(HID) * 0.5)
    u_a_w_words, u_a_w_scales = pack_weight((np.random.standard_normal((HID, HID)) * 0.6 / np.sqrt(HID)).T, FMT)
    p_a_w_words, p_a_w_scales = pack_weight((np.random.standard_normal((HID, HID)) * 0.6 / np.sqrt(HID) / p).T, FMT)
    return {"inputs": inputs,
            "state": state,
            "parent_state": parent_state,
            "c": c,
            "w_a_w_words": w_a_w_words,
            "w_a_w_scales": w_a_w_scales,
            "w_a_b": w_a_b,
            "u_a_w_words": u_a_w_words,
            "u_a_w_scales": u_a_w_scales,
            "p_a_w_words": p_a_w_words,
            "p_a_w_scales": p_a_w_scales}


def reference(inputs, state, parent_state, c, w_a_w_words, w_a_w_scales, w_a_b, u_a_w_words, u_a_w_scales, p_a_w_words, p_a_w_scales):
    st = f64(state)
    att = sigmoid(lin(mxq(f64(inputs), 1, "e4m3"), w_a_w_words, w_a_w_scales) + f64(w_a_b) + lin(mxq(st, 1, "e4m3"), u_a_w_words, u_a_w_scales) + lin(mxq(f64(parent_state), 1, "e4m3"), p_a_w_words, p_a_w_scales))
    return att * f64(c) + (1.0 - att) * st

@@ -1,0 +1,215 @@
+from contextlib import ExitStack
+
+import concourse.mybir as mybir
+from concourse.masks import make_identity
+
+F32 = mybir.dt.float32
+BF16 = mybir.dt.bfloat16
+I32 = mybir.dt.int32
+U32 = mybir.dt.uint32
+U8 = mybir.dt.uint8
+FP8X4 = mybir.dt.float8_e4m3fn_x4
+ACT = mybir.ActivationFunctionType
+ALU = mybir.AluOpType
+
+P = 128
+PACK = 4
+B = 4096
+K = 512
+N = 512
+OPERANDS = 3
+ROW_TILES = B // P
+TILES = 4
+ROUNDS = ROW_TILES // TILES
+ROUND_ROWS = TILES * P
+SLICES = N // P
+WORDS = K // 2
+LOAD_AHEAD = 3
+
+FLOPS = 2 * B * K * N * OPERANDS
+
+
+def tile_parentgru_pb_t_kernel(
+    tc,
+    inputs,
+    state,
+    parent_state,
+    c,
+    w_a_w_words,
+    w_a_w_scales,
+    w_a_b,
+    u_a_w_words,
+    u_a_w_scales,
+    p_a_w_words,
+    p_a_w_scales,
+    out,
+):
+    nc = tc.nc
+    activations = [inputs, state, parent_state]
+    weight_words = [w_a_w_words, u_a_w_words, p_a_w_words]
+    weight_scales = [w_a_w_scales, u_a_w_scales, p_a_w_scales]
+    STATE = 1
+
+    act_views = [x.rearrange("(p t) k -> p t k", t=ROW_TILES) for x in activations]
+    c_view = c.rearrange("(p t) n -> p t n", t=ROW_TILES)
+    out_view = out.rearrange("(p t) n -> p t n", t=ROW_TILES)
+
+    with ExitStack() as ctx:
+        consts = ctx.enter_context(tc.tile_pool(name="consts", bufs=1))
+        stream = ctx.enter_context(tc.tile_pool(name="stream", bufs=LOAD_AHEAD + 2))
+        work = ctx.enter_context(tc.tile_pool(name="work", bufs=2))
+        psum = ctx.enter_context(tc.psum_pool(name="psum", bufs=8))
+        ctx.enter_context(tc.manual_schedule())
+
+        act_tiles = {}
+        c_tiles = {}
+        grouped_tiles = {}
+        code_tiles = {}
+        scale_tiles = {}
+        att_t_tiles = {}
+
+        def load_activations(j):
+            rows = slice(j * TILES, (j + 1) * TILES)
+            act_tiles[j] = []
+            for o in range(OPERANDS):
+                x_sb = stream.tile([P, TILES, K], BF16, name="x_sb", tag="x%d" % o)
+                nc.sync.dma_start(out=x_sb[:], in_=act_views[o][:, rows, :])
+                act_tiles[j].append(x_sb)
+
+        def load_candidate(j):
+            rows = slice(j * TILES, (j + 1) * TILES)
+            c_sb = stream.tile([P, TILES, N], BF16, name="c_sb", tag="c")
+            nc.sync.dma_start(out=c_sb[:], in_=c_view[:, rows, :])
+            c_tiles[j] = c_sb
+
+        def transpose_in(j):
+            grouped_tiles[j] = []
+            for o in range(OPERANDS):
+                words = act_tiles[j][o][:].bitcast(F32)
+                grouped = work.tile(
+                    [P, ROUND_ROWS * PACK], BF16, name="grouped", tag="grouped%d" % o, align_bytes=64
+                )
+                grouped_words = grouped[:].bitcast(F32).rearrange("p (r u) -> p r u", u=2)
+                for half in range(TILES // 2):
+                    xt = psum.tile([P, 2, 2 * P], F32, name="xt", tag="bank")
+                    for a in range(2):
+                        for u in range(2):
+                            nc.tensor.transpose(
+                                xt[:, u, a * P : (a + 1) * P],
+                                words[:, 2 * half + a, u:WORDS:2],
+                                ident[:],
+                            )
+                    nc.scalar.copy(
+                        out=grouped_words[:, half * 2 * P : (half + 1) * 2 * P, :],
+                        in_=xt[:].rearrange("p u r -> p r u"),
+                    )
+                grouped_tiles[j].append(grouped)
+
+        def quantise(j):
+            code_tiles[j] = []
+            scale_tiles[j] = []
+            for o in range(OPERANDS):
+                codes = work.tile([P, ROUND_ROWS], U32, name="codes", tag="codes%d" % o, align_bytes=64)
+                scales = work.tile([P, ROUND_ROWS], U8, name="scales", tag="scales%d" % o, align_bytes=64)
+                nc.vector.quantize_mx(
+                    out=codes[:].bitcast(FP8X4), scales=scales[:], in_=grouped_tiles[j][o][:]
+                )
+                code_tiles[j].append(codes)
+                scale_tiles[j].append(scales)
+
+        def gates(j):
+            att_t = work.tile([P, SLICES, ROUND_ROWS], F32, name="att_t", tag="att_t")
+            for s in range(SLICES):
+                z = psum.tile([P, ROUND_ROWS], F32, name="z", tag="bank")
+                for o in range(OPERANDS):
+                    nc.tensor.matmul_mx(
+                        out=z[:],
+                        lhsT=w_bytes[o][:, s * P * PACK : (s + 1) * P * PACK].bitcast(FP8X4),
+                        lhsT_scale=w_planes[:, o, s * P : (s + 1) * P],
+                        rhs=code_tiles[j][o][:].bitcast(FP8X4),
+                        rhs_scale=scale_tiles[j][o][:],
+                        start=(o == 0),
+                        stop=(o == OPERANDS - 1),
+                    )
+                nc.scalar.activation(
+                    out=att_t[:, s, :], in_=z[:], func=ACT.Sigmoid, bias=bias_sb[:, s : s + 1]
+                )
+            att_t_tiles[j] = att_t
+
+        def blend(j):
+            rows = slice(j * TILES, (j + 1) * TILES)
+            att_c = work.tile([P, TILES, N], F32, name="att_c", tag="att_c")
+            att_s = work.tile([P, TILES, N], F32, name="att_s", tag="att_s")
+            result = work.tile([P, TILES, N], F32, name="result", tag="result")
+            for a in range(TILES):
+                att = psum.tile([P, N], F32, name="att", tag="bank")
+                for s in range(SLICES):
+                    nc.tensor.transpose(
+                        att[:, s * P : (s + 1) * P],
+                        att_t_tiles[j][:, s, a * P : (a + 1) * P],
+                        ident[:],
+                    )
+                nc.vector.tensor_tensor(
+                    out=att_c[:, a, :], in0=att[:], in1=c_tiles[j][:, a, :], op=ALU.mult
+                )
+                nc.vector.scalar_tensor_tensor(
+                    out=att_s[:, a, :],
+                    in0=att[:],
+                    scalar=-1.0,
+                    in1=act_tiles[j][STATE][:, a, :],
+                    op0=ALU.add,
+                    op1=ALU.mult,
+                )
+                nc.gpsimd.tensor_tensor(
+                    out=result[:, a, :], in0=att_c[:, a, :], in1=att_s[:, a, :], op=ALU.subtract
+                )
+            nc.sync.dma_start(out=out_view[:, rows, :], in_=result[:])
+
+        w_planes = consts.tile([P, OPERANDS, N], U8, name="w_planes", align_bytes=64)
+        nc.vector.memset(w_planes[:].bitcast(I32), 0)
+        bias_rows = consts.tile([P, P], BF16, name="bias_rows")
+        nc.vector.memset(bias_rows[:], 0.0)
+        nc.sync.dma_start(out=bias_rows[0:SLICES, :], in_=w_a_b.rearrange("(s m) -> s m", m=P))
+        warm_in = consts.tile([P, 1], F32, name="warm_in")
+        warm_out = consts.tile([P, 1], F32, name="warm_out")
+        nc.vector.memset(warm_in[:], 0.0)
+        nc.scalar.activation(out=warm_out[:], in_=warm_in[:], func=ACT.Sigmoid)
+        ident = consts.tile([P, P], F32, name="ident")
+        make_identity(nc, ident[:])
+
+        load_activations(0)
+        for o in range(OPERANDS):
+            for r in range(4):
+                nc.sync.dma_start(
+                    out=w_planes[r:P:32, o, :].bitcast(I32),
+                    in_=weight_scales[o][0, r:16:4, :].bitcast(I32),
+                )
+        w_bytes = []
+        for o in range(OPERANDS):
+            w_sb = consts.tile([P, N * PACK], U8, name="w_sb%d" % o, align_bytes=64)
+            nc.sync.dma_start(
+                out=w_sb[:].bitcast(I32),
+                in_=weight_words[o].rearrange("g p n t -> (g p) (n t)").bitcast(I32),
+            )
+            w_bytes.append(w_sb)
+        load_activations(1)
+
+        bias_rows_f32 = consts.tile([P, P], F32, name="bias_rows_f32")
+        bias_sb = consts.tile([P, SLICES], F32, name="bias_sb")
+        nc.vector.tensor_copy(out=bias_rows_f32[:], in_=bias_rows[:])
+        bias_t = psum.tile([P, N], F32, name="bias_t", tag="bank")
+        nc.tensor.transpose(bias_t[:, 0:P], bias_rows_f32[:], ident[:])
+        nc.vector.tensor_copy(out=bias_sb[:], in_=bias_t[:, 0:SLICES])
+
+        for j in range(-1, ROUNDS + 1):
+            if j + LOAD_AHEAD < ROUNDS:
+                load_activations(j + LOAD_AHEAD)
+            if j + 1 < ROUNDS:
+                load_candidate(j + 1)
+                transpose_in(j + 1)
+            if j - 1 >= 0:
+                blend(j - 1)
+            if j + 1 < ROUNDS:
+                quantise(j + 1)
+            if 0 <= j < ROUNDS:
+                gates(j)

@@ -18,12 +18,17 @@ B = 4096
 K = 512
 N = 512
 OPERANDS = 3
+STATE = 1
 ROW_TILES = B // P
 TILES = 4
 ROUNDS = ROW_TILES // TILES
 ROUND_ROWS = TILES * P
 SLICES = N // P
 WORDS = K // 2
+STEP_TILES = 1
+STEPS = TILES // STEP_TILES
+ALL_STEPS = ROUNDS * STEPS
+OUT_LAG = STEPS + 1
 LOAD_AHEAD = 3
 
 FLOPS = 2 * B * K * N * OPERANDS
@@ -48,7 +53,6 @@ def tile_parentgru_pb_t_kernel(
     activations = [inputs, state, parent_state]
     weight_words = [w_a_w_words, u_a_w_words, p_a_w_words]
     weight_scales = [w_a_w_scales, u_a_w_scales, p_a_w_scales]
-    STATE = 1
 
     act_views = [x.rearrange("(p t) k -> p t k", t=ROW_TILES) for x in activations]
     c_view = c.rearrange("(p t) n -> p t n", t=ROW_TILES)
@@ -56,9 +60,10 @@ def tile_parentgru_pb_t_kernel(
 
     with ExitStack() as ctx:
         consts = ctx.enter_context(tc.tile_pool(name="consts", bufs=1))
-        stream = ctx.enter_context(tc.tile_pool(name="stream", bufs=LOAD_AHEAD + 2))
+        stream = ctx.enter_context(tc.tile_pool(name="stream", bufs=2 * LOAD_AHEAD))
         work = ctx.enter_context(tc.tile_pool(name="work", bufs=2))
-        psum = ctx.enter_context(tc.psum_pool(name="psum", bufs=8))
+        leave = ctx.enter_context(tc.tile_pool(name="leave", bufs=3))
+        psum = ctx.enter_context(tc.psum_pool(name="psum", bufs=2))
         ctx.enter_context(tc.manual_schedule())
 
         act_tiles = {}
@@ -82,45 +87,57 @@ def tile_parentgru_pb_t_kernel(
             nc.sync.dma_start(out=c_sb[:], in_=c_view[:, rows, :])
             c_tiles[j] = c_sb
 
-        def transpose_in(j):
-            grouped_tiles[j] = []
+        def transpose_in(step):
+            j, part = divmod(step, STEPS)
+            if part == 0:
+                grouped_tiles[j] = [
+                    work.tile(
+                        [P, ROUND_ROWS * PACK], BF16, name="grouped", tag="grouped%d" % o, align_bytes=64
+                    )
+                    for o in range(OPERANDS)
+                ]
+            first = part * STEP_TILES
             for o in range(OPERANDS):
                 words = act_tiles[j][o][:].bitcast(F32)
-                grouped = work.tile(
-                    [P, ROUND_ROWS * PACK], BF16, name="grouped", tag="grouped%d" % o, align_bytes=64
+                grouped_words = grouped_tiles[j][o][:].bitcast(F32).rearrange("p (r u) -> p r u", u=2)
+                xt = psum.tile([P, 2, STEP_TILES * P], F32, name="xt", tag="xt", bufs=4)
+                for a in range(STEP_TILES):
+                    for u in range(2):
+                        nc.tensor.transpose(
+                            xt[:, u, a * P : (a + 1) * P], words[:, first + a, u:WORDS:2], ident[:]
+                        )
+                nc.scalar.copy(
+                    out=grouped_words[:, first * P : (first + STEP_TILES) * P, :],
+                    in_=xt[:].rearrange("p u r -> p r u"),
                 )
-                grouped_words = grouped[:].bitcast(F32).rearrange("p (r u) -> p r u", u=2)
-                for half in range(TILES // 2):
-                    xt = psum.tile([P, 2, 2 * P], F32, name="xt", tag="bank")
-                    for a in range(2):
-                        for u in range(2):
-                            nc.tensor.transpose(
-                                xt[:, u, a * P : (a + 1) * P],
-                                words[:, 2 * half + a, u:WORDS:2],
-                                ident[:],
-                            )
-                    nc.scalar.copy(
-                        out=grouped_words[:, half * 2 * P : (half + 1) * 2 * P, :],
-                        in_=xt[:].rearrange("p u r -> p r u"),
-                    )
-                grouped_tiles[j].append(grouped)
 
-        def quantise(j):
-            code_tiles[j] = []
-            scale_tiles[j] = []
+        def quantise(step):
+            j, part = divmod(step, STEPS)
+            if part == 0:
+                code_tiles[j] = [
+                    work.tile([P, ROUND_ROWS], U32, name="codes", tag="codes%d" % o, align_bytes=64)
+                    for o in range(OPERANDS)
+                ]
+                scale_tiles[j] = [
+                    work.tile([P, ROUND_ROWS], U8, name="scales", tag="scales%d" % o, align_bytes=64)
+                    for o in range(OPERANDS)
+                ]
+            first_row = part * STEP_TILES * P
+            rows = slice(first_row, first_row + STEP_TILES * P)
+            values = slice(first_row * PACK, (first_row + STEP_TILES * P) * PACK)
             for o in range(OPERANDS):
-                codes = work.tile([P, ROUND_ROWS], U32, name="codes", tag="codes%d" % o, align_bytes=64)
-                scales = work.tile([P, ROUND_ROWS], U8, name="scales", tag="scales%d" % o, align_bytes=64)
                 nc.vector.quantize_mx(
-                    out=codes[:].bitcast(FP8X4), scales=scales[:], in_=grouped_tiles[j][o][:]
+                    out=code_tiles[j][o][:, rows].bitcast(FP8X4),
+                    scales=scale_tiles[j][o][:, rows],
+                    in_=grouped_tiles[j][o][:, values],
                 )
-                code_tiles[j].append(codes)
-                scale_tiles[j].append(scales)
 
-        def gates(j):
-            att_t = work.tile([P, SLICES, ROUND_ROWS], F32, name="att_t", tag="att_t")
-            for s in range(SLICES):
-                z = psum.tile([P, ROUND_ROWS], F32, name="z", tag="bank")
+        def gates(step):
+            j, part = divmod(step, STEPS)
+            if part == 0:
+                att_t_tiles[j] = work.tile([P, SLICES, ROUND_ROWS], F32, name="att_t", tag="att_t")
+            for s in range(part * STEP_TILES, (part + 1) * STEP_TILES):
+                z = psum.tile([P, ROUND_ROWS], F32, name="z", tag="z")
                 for o in range(OPERANDS):
                     nc.tensor.matmul_mx(
                         out=z[:],
@@ -132,28 +149,27 @@ def tile_parentgru_pb_t_kernel(
                         stop=(o == OPERANDS - 1),
                     )
                 nc.scalar.activation(
-                    out=att_t[:, s, :], in_=z[:], func=ACT.Sigmoid, bias=bias_sb[:, s : s + 1]
+                    out=att_t_tiles[j][:, s, :], in_=z[:], func=ACT.Sigmoid, bias=bias_sb[:, s : s + 1]
                 )
-            att_t_tiles[j] = att_t
 
-        def blend(j):
-            rows = slice(j * TILES, (j + 1) * TILES)
-            att_c = work.tile([P, TILES, N], F32, name="att_c", tag="att_c")
-            att_s = work.tile([P, TILES, N], F32, name="att_s", tag="att_s")
-            result = work.tile([P, TILES, N], F32, name="result", tag="result")
-            for a in range(TILES):
-                att = psum.tile([P, N], F32, name="att", tag="bank")
+        def blend(step):
+            j, part = divmod(step, STEPS)
+            first = part * STEP_TILES
+            att_c = leave.tile([P, STEP_TILES, N], F32, name="att_c", tag="att_c")
+            att_s = leave.tile([P, STEP_TILES, N], F32, name="att_s", tag="att_s")
+            result = leave.tile([P, STEP_TILES, N], F32, name="result", tag="result")
+            for i in range(STEP_TILES):
+                a = first + i
+                att = psum.tile([P, N], F32, name="att", tag="att")
                 for s in range(SLICES):
                     nc.tensor.transpose(
-                        att[:, s * P : (s + 1) * P],
-                        att_t_tiles[j][:, s, a * P : (a + 1) * P],
-                        ident[:],
+                        att[:, s * P : (s + 1) * P], att_t_tiles[j][:, s, a * P : (a + 1) * P], ident[:]
                     )
                 nc.vector.tensor_tensor(
-                    out=att_c[:, a, :], in0=att[:], in1=c_tiles[j][:, a, :], op=ALU.mult
+                    out=att_c[:, i, :], in0=att[:], in1=c_tiles[j][:, a, :], op=ALU.mult
                 )
                 nc.vector.scalar_tensor_tensor(
-                    out=att_s[:, a, :],
+                    out=att_s[:, i, :],
                     in0=att[:],
                     scalar=-1.0,
                     in1=act_tiles[j][STATE][:, a, :],
@@ -161,9 +177,10 @@ def tile_parentgru_pb_t_kernel(
                     op1=ALU.mult,
                 )
                 nc.gpsimd.tensor_tensor(
-                    out=result[:, a, :], in0=att_c[:, a, :], in1=att_s[:, a, :], op=ALU.subtract
+                    out=result[:, i, :], in0=att_c[:, i, :], in1=att_s[:, i, :], op=ALU.subtract
                 )
-            nc.sync.dma_start(out=out_view[:, rows, :], in_=result[:])
+            tiles = slice(j * TILES + first, j * TILES + first + STEP_TILES)
+            nc.sync.dma_start(out=out_view[:, tiles, :], in_=result[:])
 
         w_planes = consts.tile([P, OPERANDS, N], U8, name="w_planes", align_bytes=64)
         nc.vector.memset(w_planes[:].bitcast(I32), 0)
@@ -197,19 +214,21 @@ def tile_parentgru_pb_t_kernel(
         bias_rows_f32 = consts.tile([P, P], F32, name="bias_rows_f32")
         bias_sb = consts.tile([P, SLICES], F32, name="bias_sb")
         nc.vector.tensor_copy(out=bias_rows_f32[:], in_=bias_rows[:])
-        bias_t = psum.tile([P, N], F32, name="bias_t", tag="bank")
+        bias_t = psum.tile([P, N], F32, name="bias_t", tag="att")
         nc.tensor.transpose(bias_t[:, 0:P], bias_rows_f32[:], ident[:])
         nc.vector.tensor_copy(out=bias_sb[:], in_=bias_t[:, 0:SLICES])
 
-        for j in range(-1, ROUNDS + 1):
-            if j + LOAD_AHEAD < ROUNDS:
+        for step in range(-STEPS, ALL_STEPS + OUT_LAG):
+            j, part = divmod(step, STEPS)
+            if part == 0 and j + LOAD_AHEAD < ROUNDS:
                 load_activations(j + LOAD_AHEAD)
-            if j + 1 < ROUNDS:
+            if part == 0 and j + 1 < ROUNDS:
                 load_candidate(j + 1)
-                transpose_in(j + 1)
-            if j - 1 >= 0:
-                blend(j - 1)
-            if j + 1 < ROUNDS:
-                quantise(j + 1)
-            if 0 <= j < ROUNDS:
-                gates(j)
+            if step + STEPS < ALL_STEPS:
+                transpose_in(step + STEPS)
+            if step - OUT_LAG >= 0:
+                blend(step - OUT_LAG)
+            if step + STEPS < ALL_STEPS:
+                quantise(step + STEPS)
+            if 0 <= step < ALL_STEPS:
+                gates(step)

@@ -28,8 +28,10 @@ WORDS = K // 2
 STEP_TILES = 1
 STEPS = TILES // STEP_TILES
 ALL_STEPS = ROUNDS * STEPS
-OUT_LAG = STEPS + 1
-LOAD_AHEAD = 3
+IN_LEAD = 2 * STEPS
+OUT_LAG = 2
+LOAD_AHEAD = 4
+LOAD_TILES = 2
 
 FLOPS = 2 * B * K * N * OPERANDS
 
@@ -60,9 +62,8 @@ def tile_parentgru_pb_t_kernel(
 
     with ExitStack() as ctx:
         consts = ctx.enter_context(tc.tile_pool(name="consts", bufs=1))
-        stream = ctx.enter_context(tc.tile_pool(name="stream", bufs=2 * LOAD_AHEAD))
-        work = ctx.enter_context(tc.tile_pool(name="work", bufs=2))
-        leave = ctx.enter_context(tc.tile_pool(name="leave", bufs=3))
+        stream = ctx.enter_context(tc.tile_pool(name="stream", bufs=3))
+        work = ctx.enter_context(tc.tile_pool(name="work", bufs=3))
         psum = ctx.enter_context(tc.psum_pool(name="psum", bufs=2))
         ctx.enter_context(tc.manual_schedule())
 
@@ -72,19 +73,25 @@ def tile_parentgru_pb_t_kernel(
         code_tiles = {}
         scale_tiles = {}
         att_t_tiles = {}
+        result_tiles = {}
 
         def load_activations(j):
-            rows = slice(j * TILES, (j + 1) * TILES)
-            act_tiles[j] = []
-            for o in range(OPERANDS):
-                x_sb = stream.tile([P, TILES, K], BF16, name="x_sb", tag="x%d" % o)
-                nc.sync.dma_start(out=x_sb[:], in_=act_views[o][:, rows, :])
-                act_tiles[j].append(x_sb)
+            act_tiles[j] = [
+                stream.tile(
+                    [P, TILES, K], BF16, name="x_sb", tag="x%d" % o, bufs=(6 if o == STATE else 3)
+                )
+                for o in range(OPERANDS)
+            ]
+            for first in range(0, TILES, LOAD_TILES):
+                for o in range(OPERANDS):
+                    nc.sync.dma_start(
+                        out=act_tiles[j][o][:, first : first + LOAD_TILES, :],
+                        in_=act_views[o][:, j * TILES + first : j * TILES + first + LOAD_TILES, :],
+                    )
 
         def load_candidate(j):
-            rows = slice(j * TILES, (j + 1) * TILES)
             c_sb = stream.tile([P, TILES, N], BF16, name="c_sb", tag="c")
-            nc.sync.dma_start(out=c_sb[:], in_=c_view[:, rows, :])
+            nc.sync.dma_start(out=c_sb[:], in_=c_view[:, j * TILES : (j + 1) * TILES, :])
             c_tiles[j] = c_sb
 
         def transpose_in(step):
@@ -134,8 +141,6 @@ def tile_parentgru_pb_t_kernel(
 
         def gates(step):
             j, part = divmod(step, STEPS)
-            if part == 0:
-                att_t_tiles[j] = work.tile([P, SLICES, ROUND_ROWS], F32, name="att_t", tag="att_t")
             for s in range(part * STEP_TILES, (part + 1) * STEP_TILES):
                 z = psum.tile([P, ROUND_ROWS], F32, name="z", tag="z")
                 for o in range(OPERANDS):
@@ -148,39 +153,35 @@ def tile_parentgru_pb_t_kernel(
                         start=(o == 0),
                         stop=(o == OPERANDS - 1),
                     )
-                nc.scalar.activation(
-                    out=att_t_tiles[j][:, s, :], in_=z[:], func=ACT.Sigmoid, bias=bias_sb[:, s : s + 1]
-                )
+                att_t = work.tile([P, ROUND_ROWS], F32, name="att_t", tag="att_t", bufs=4 * STEP_TILES)
+                nc.scalar.activation(out=att_t[:], in_=z[:], func=ACT.Sigmoid, bias=bias_sb[:, s : s + 1])
+                att_t_tiles[(j, s)] = att_t
 
         def blend(step):
             j, part = divmod(step, STEPS)
-            first = part * STEP_TILES
-            att_c = leave.tile([P, STEP_TILES, N], F32, name="att_c", tag="att_c")
-            att_s = leave.tile([P, STEP_TILES, N], F32, name="att_s", tag="att_s")
-            result = leave.tile([P, STEP_TILES, N], F32, name="result", tag="result")
-            for i in range(STEP_TILES):
-                a = first + i
-                att = psum.tile([P, N], F32, name="att", tag="att")
-                for s in range(SLICES):
-                    nc.tensor.transpose(
-                        att[:, s * P : (s + 1) * P], att_t_tiles[j][:, s, a * P : (a + 1) * P], ident[:]
-                    )
-                nc.vector.tensor_tensor(
-                    out=att_c[:, i, :], in0=att[:], in1=c_tiles[j][:, a, :], op=ALU.mult
-                )
+            if part == 0:
+                result_tiles[j] = work.tile([P, TILES, N], F32, name="result", tag="result", bufs=2)
+            for s in range(part * STEP_TILES, (part + 1) * STEP_TILES):
+                features = slice(s * P, (s + 1) * P)
+                att = psum.tile([P, TILES, P], F32, name="att", tag="att")
+                for a in range(TILES):
+                    nc.tensor.transpose(att[:, a, :], att_t_tiles[(j, s)][:, a * P : (a + 1) * P], ident[:])
+                att_c = work.tile([P, TILES, P], F32, name="att_c", tag="att_c")
+                att_s = work.tile([P, TILES, P], F32, name="att_s", tag="att_s")
+                nc.vector.tensor_tensor(out=att_c[:], in0=att[:], in1=c_tiles[j][:, :, features], op=ALU.mult)
                 nc.vector.scalar_tensor_tensor(
-                    out=att_s[:, i, :],
+                    out=att_s[:],
                     in0=att[:],
                     scalar=-1.0,
-                    in1=act_tiles[j][STATE][:, a, :],
+                    in1=act_tiles[j][STATE][:, :, features],
                     op0=ALU.add,
                     op1=ALU.mult,
                 )
                 nc.gpsimd.tensor_tensor(
-                    out=result[:, i, :], in0=att_c[:, i, :], in1=att_s[:, i, :], op=ALU.subtract
+                    out=result_tiles[j][:, :, features], in0=att_c[:], in1=att_s[:], op=ALU.subtract
                 )
-            tiles = slice(j * TILES + first, j * TILES + first + STEP_TILES)
-            nc.sync.dma_start(out=out_view[:, tiles, :], in_=result[:])
+            if part == STEPS - 1:
+                nc.sync.dma_start(out=out_view[:, j * TILES : (j + 1) * TILES, :], in_=result_tiles[j][:])
 
         w_planes = consts.tile([P, OPERANDS, N], U8, name="w_planes", align_bytes=64)
         nc.vector.memset(w_planes[:].bitcast(I32), 0)
@@ -194,13 +195,14 @@ def tile_parentgru_pb_t_kernel(
         ident = consts.tile([P, P], F32, name="ident")
         make_identity(nc, ident[:])
 
-        load_activations(0)
         for o in range(OPERANDS):
             for r in range(4):
-                nc.sync.dma_start(
-                    out=w_planes[r:P:32, o, :].bitcast(I32),
-                    in_=weight_scales[o][0, r:16:4, :].bitcast(I32),
+                nc.gpsimd.dma_start(
+                    out=w_planes[r:P:32, o, :].bitcast(F32),
+                    in_=weight_scales[o][0, r:16:4, :].bitcast(F32),
                 )
+        load_activations(0)
+        load_activations(1)
         w_bytes = []
         for o in range(OPERANDS):
             w_sb = consts.tile([P, N * PACK], U8, name="w_sb%d" % o, align_bytes=64)
@@ -209,7 +211,6 @@ def tile_parentgru_pb_t_kernel(
                 in_=weight_words[o].rearrange("g p n t -> (g p) (n t)").bitcast(I32),
             )
             w_bytes.append(w_sb)
-        load_activations(1)
 
         bias_rows_f32 = consts.tile([P, P], F32, name="bias_rows_f32")
         bias_sb = consts.tile([P, SLICES], F32, name="bias_sb")
@@ -218,17 +219,17 @@ def tile_parentgru_pb_t_kernel(
         nc.tensor.transpose(bias_t[:, 0:P], bias_rows_f32[:], ident[:])
         nc.vector.tensor_copy(out=bias_sb[:], in_=bias_t[:, 0:SLICES])
 
-        for step in range(-STEPS, ALL_STEPS + OUT_LAG):
+        for step in range(-IN_LEAD, ALL_STEPS + OUT_LAG):
             j, part = divmod(step, STEPS)
+            if part == 0 and 0 <= j + 1 < ROUNDS:
+                load_candidate(j + 1)
             if part == 0 and j + LOAD_AHEAD < ROUNDS:
                 load_activations(j + LOAD_AHEAD)
-            if part == 0 and j + 1 < ROUNDS:
-                load_candidate(j + 1)
-            if step + STEPS < ALL_STEPS:
-                transpose_in(step + STEPS)
+            if step + IN_LEAD < ALL_STEPS:
+                transpose_in(step + IN_LEAD)
             if step - OUT_LAG >= 0:
                 blend(step - OUT_LAG)
-            if step + STEPS < ALL_STEPS:
-                quantise(step + STEPS)
+            if step + IN_LEAD < ALL_STEPS:
+                quantise(step + IN_LEAD)
             if 0 <= step < ALL_STEPS:
                 gates(step)

@@ -28,9 +28,9 @@ WORDS = K // 2
 STEP_TILES = 1
 STEPS = TILES // STEP_TILES
 ALL_STEPS = ROUNDS * STEPS
-IN_LEAD = 2 * STEPS
+IN_LEAD = STEPS + 1
 OUT_LAG = 2
-LOAD_AHEAD = 4
+LOAD_AHEAD = 3
 LOAD_TILES = 2
 
 FLOPS = 2 * B * K * N * OPERANDS
@@ -78,7 +78,7 @@ def tile_parentgru_pb_t_kernel(
         def load_activations(j):
             act_tiles[j] = [
                 stream.tile(
-                    [P, TILES, K], BF16, name="x_sb", tag="x%d" % o, bufs=(6 if o == STATE else 3)
+                    [P, TILES, K], BF16, name="x_sb", tag="x%d" % o, bufs=(5 if o == STATE else 3)
                 )
                 for o in range(OPERANDS)
             ]
@@ -195,14 +195,13 @@ def tile_parentgru_pb_t_kernel(
         ident = consts.tile([P, P], F32, name="ident")
         make_identity(nc, ident[:])
 
+        load_activations(0)
         for o in range(OPERANDS):
             for r in range(4):
-                nc.gpsimd.dma_start(
-                    out=w_planes[r:P:32, o, :].bitcast(F32),
-                    in_=weight_scales[o][0, r:16:4, :].bitcast(F32),
+                nc.sync.dma_start(
+                    out=w_planes[r:P:32, o, :].bitcast(I32),
+                    in_=weight_scales[o][0, r:16:4, :].bitcast(I32),
                 )
-        load_activations(0)
-        load_activations(1)
         w_bytes = []
         for o in range(OPERANDS):
             w_sb = consts.tile([P, N * PACK], U8, name="w_sb%d" % o, align_bytes=64)
@@ -211,6 +210,7 @@ def tile_parentgru_pb_t_kernel(
                 in_=weight_words[o].rearrange("g p n t -> (g p) (n t)").bitcast(I32),
             )
             w_bytes.append(w_sb)
+        load_activations(1)
 
         bias_rows_f32 = consts.tile([P, P], F32, name="bias_rows_f32")
         bias_sb = consts.tile([P, SLICES], F32, name="bias_sb")

@@ -18,7 +18,7 @@ B = 4096
 K = 512
 N = 512
 OPERANDS = 3
-STATE = 1
+STATE, PARENT = 1, 2
 ROW_TILES = B // P
 TILES = 4
 ROUNDS = ROW_TILES // TILES
@@ -29,6 +29,8 @@ STEP_TILES = 1
 STEPS = TILES // STEP_TILES
 ALL_STEPS = ROUNDS * STEPS
 IN_LEAD = STEPS + 1
+SORT_AHEAD = 2
+UNSORTED_STEPS = 4
 OUT_LAG = 2
 LOAD_AHEAD = 3
 LOAD_TILES = 2
@@ -69,6 +71,7 @@ def tile_parentgru_pb_t_kernel(
 
         act_tiles = {}
         c_tiles = {}
+        sorted_tiles = {}
         grouped_tiles = {}
         code_tiles = {}
         scale_tiles = {}
@@ -94,28 +97,37 @@ def tile_parentgru_pb_t_kernel(
             nc.sync.dma_start(out=c_sb[:], in_=c_view[:, j * TILES : (j + 1) * TILES, :])
             c_tiles[j] = c_sb
 
+        def sort_words(step):
+            if not UNSORTED_STEPS <= step < ALL_STEPS:
+                return
+            j, t = divmod(step, TILES)
+            for o, copy in ((STATE, nc.scalar.copy), (PARENT, nc.vector.tensor_copy)):
+                words = act_tiles[j][o][:, t, :].bitcast(F32)
+                sorted_words = work.tile([P, 2, P], F32, name="sorted_words", tag="sorted%d" % o, bufs=4)
+                copy(out=sorted_words[:], in_=words.rearrange("p (w u) -> p u w", u=2))
+                sorted_tiles[(step, o)] = sorted_words
+
         def transpose_in(step):
-            j, part = divmod(step, STEPS)
-            if part == 0:
+            j, t = divmod(step, TILES)
+            if t == 0:
                 grouped_tiles[j] = [
                     work.tile(
                         [P, ROUND_ROWS * PACK], BF16, name="grouped", tag="grouped%d" % o, align_bytes=64
                     )
                     for o in range(OPERANDS)
                 ]
-            first = part * STEP_TILES
             for o in range(OPERANDS):
-                words = act_tiles[j][o][:].bitcast(F32)
+                words = act_tiles[j][o][:, t, :].bitcast(F32)
                 grouped_words = grouped_tiles[j][o][:].bitcast(F32).rearrange("p (r u) -> p r u", u=2)
-                xt = psum.tile([P, 2, STEP_TILES * P], F32, name="xt", tag="xt", bufs=4)
-                for a in range(STEP_TILES):
-                    for u in range(2):
-                        nc.tensor.transpose(
-                            xt[:, u, a * P : (a + 1) * P], words[:, first + a, u:WORDS:2], ident[:]
-                        )
+                xt = psum.tile([P, 2, P], F32, name="xt", tag="xt", bufs=4)
+                for u in range(2):
+                    if (step, o) in sorted_tiles:
+                        source = sorted_tiles[(step, o)][:, u, :]
+                    else:
+                        source = words[:, u:WORDS:2]
+                    nc.tensor.transpose(xt[:, u, :], source, ident[:])
                 nc.scalar.copy(
-                    out=grouped_words[:, first * P : (first + STEP_TILES) * P, :],
-                    in_=xt[:].rearrange("p u r -> p r u"),
+                    out=grouped_words[:, t * P : (t + 1) * P, :], in_=xt[:].rearrange("p u r -> p r u")
                 )
 
         def quantise(step):
@@ -219,11 +231,13 @@ def tile_parentgru_pb_t_kernel(
         nc.tensor.transpose(bias_t[:, 0:P], bias_rows_f32[:], ident[:])
         nc.vector.tensor_copy(out=bias_sb[:], in_=bias_t[:, 0:SLICES])
 
+        load_candidate(0)
+        load_activations(2)
         for step in range(-IN_LEAD, ALL_STEPS + OUT_LAG):
             j, part = divmod(step, STEPS)
-            if part == 0 and 0 <= j + 1 < ROUNDS:
+            if part == 0 and 0 <= j < ROUNDS - 1:
                 load_candidate(j + 1)
-            if part == 0 and j + LOAD_AHEAD < ROUNDS:
+            if part == 0 and 0 <= j < ROUNDS - LOAD_AHEAD:
                 load_activations(j + LOAD_AHEAD)
             if step + IN_LEAD < ALL_STEPS:
                 transpose_in(step + IN_LEAD)
@@ -233,3 +247,4 @@ def tile_parentgru_pb_t_kernel(
                 quantise(step + IN_LEAD)
             if 0 <= step < ALL_STEPS:
                 gates(step)
+            sort_words(step + IN_LEAD + SORT_AHEAD)

@@ -18,7 +18,8 @@ B = 4096
 K = 512
 N = 512
 OPERANDS = 3
-STATE, PARENT = 1, 2
+STATE = 1
+SORTED = (STATE,)
 ROW_TILES = B // P
 TILES = 4
 ROUNDS = ROW_TILES // TILES
@@ -30,7 +31,7 @@ STEPS = TILES // STEP_TILES
 ALL_STEPS = ROUNDS * STEPS
 IN_LEAD = STEPS + 1
 SORT_AHEAD = 2
-UNSORTED_STEPS = 4
+UNSORTED_STEPS = 8
 OUT_LAG = 2
 LOAD_AHEAD = 3
 LOAD_TILES = 2
@@ -101,10 +102,10 @@ def tile_parentgru_pb_t_kernel(
             if not UNSORTED_STEPS <= step < ALL_STEPS:
                 return
             j, t = divmod(step, TILES)
-            for o, copy in ((STATE, nc.scalar.copy), (PARENT, nc.vector.tensor_copy)):
+            for o in SORTED:
                 words = act_tiles[j][o][:, t, :].bitcast(F32)
                 sorted_words = work.tile([P, 2, P], F32, name="sorted_words", tag="sorted%d" % o, bufs=4)
-                copy(out=sorted_words[:], in_=words.rearrange("p (w u) -> p u w", u=2))
+                nc.scalar.copy(out=sorted_words[:], in_=words.rearrange("p (w u) -> p u w", u=2))
                 sorted_tiles[(step, o)] = sorted_words
 
         def transpose_in(step):
@@ -189,10 +190,16 @@ def tile_parentgru_pb_t_kernel(
                     op0=ALU.add,
                     op1=ALU.mult,
                 )
-                nc.gpsimd.tensor_tensor(
+                last = j == ROUNDS - 1
+                engine = nc.vector if last and s == SLICES - 1 else nc.gpsimd
+                engine.tensor_tensor(
                     out=result_tiles[j][:, :, features], in0=att_c[:], in1=att_s[:], op=ALU.subtract
                 )
-            if part == STEPS - 1:
+                if last:
+                    nc.sync.dma_start(
+                        out=out_view[:, j * TILES : (j + 1) * TILES, features], in_=result_tiles[j][:, :, features]
+                    )
+            if part == STEPS - 1 and j < ROUNDS - 1:
                 nc.sync.dma_start(out=out_view[:, j * TILES : (j + 1) * TILES, :], in_=result_tiles[j][:])
 
         w_planes = consts.tile([P, OPERANDS, N], U8, name="w_planes", align_bytes=64)

@@ -19,22 +19,20 @@ K = 512
 N = 512
 OPERANDS = 3
 STATE = 1
-SORTED = (STATE,)
 ROW_TILES = B // P
 TILES = 4
 ROUNDS = ROW_TILES // TILES
 ROUND_ROWS = TILES * P
 SLICES = N // P
 WORDS = K // 2
-STEP_TILES = 1
-STEPS = TILES // STEP_TILES
+STEPS = SLICES
 ALL_STEPS = ROUNDS * STEPS
-IN_LEAD = STEPS + 1
-SORT_AHEAD = 2
-UNSORTED_STEPS = 8
+UNITS = OPERANDS * TILES
+STEP_UNITS = UNITS // STEPS
+IN_LEAD = 4
+QUANTISE_LAG = 2
 OUT_LAG = 2
 LOAD_AHEAD = 3
-LOAD_TILES = 2
 
 FLOPS = 2 * B * K * N * OPERANDS
 
@@ -72,101 +70,70 @@ def tile_parentgru_pb_t_kernel(
 
         act_tiles = {}
         c_tiles = {}
-        sorted_tiles = {}
         grouped_tiles = {}
         code_tiles = {}
         scale_tiles = {}
         att_t_tiles = {}
         result_tiles = {}
 
-        def load_activations(j):
-            act_tiles[j] = [
-                stream.tile(
-                    [P, TILES, K], BF16, name="x_sb", tag="x%d" % o, bufs=(5 if o == STATE else 3)
+        def load_activation(j, o, parts=1):
+            x_sb = stream.tile([P, TILES, K], BF16, name="x_sb", tag="x%d" % o, bufs=(6 if o == STATE else 4))
+            size = TILES // parts
+            for first in range(0, TILES, size):
+                nc.sync.dma_start(
+                    out=x_sb[:, first : first + size, :],
+                    in_=act_views[o][:, j * TILES + first : j * TILES + first + size, :],
                 )
-                for o in range(OPERANDS)
-            ]
-            for first in range(0, TILES, LOAD_TILES):
-                for o in range(OPERANDS):
-                    nc.sync.dma_start(
-                        out=act_tiles[j][o][:, first : first + LOAD_TILES, :],
-                        in_=act_views[o][:, j * TILES + first : j * TILES + first + LOAD_TILES, :],
-                    )
+            act_tiles[(j, o)] = x_sb
+
+        def load_activations(j, parts=1):
+            for o in range(OPERANDS):
+                load_activation(j, o, parts)
 
         def load_candidate(j):
             c_sb = stream.tile([P, TILES, N], BF16, name="c_sb", tag="c")
             nc.sync.dma_start(out=c_sb[:], in_=c_view[:, j * TILES : (j + 1) * TILES, :])
             c_tiles[j] = c_sb
 
-        def sort_words(step):
-            if not UNSORTED_STEPS <= step < ALL_STEPS:
-                return
-            j, t = divmod(step, TILES)
-            for o in SORTED:
-                words = act_tiles[j][o][:, t, :].bitcast(F32)
-                sorted_words = work.tile([P, 2, P], F32, name="sorted_words", tag="sorted%d" % o, bufs=4)
-                nc.scalar.copy(out=sorted_words[:], in_=words.rearrange("p (w u) -> p u w", u=2))
-                sorted_tiles[(step, o)] = sorted_words
-
-        def transpose_in(step):
-            j, t = divmod(step, TILES)
+        def transpose_in(unit):
+            j, r = divmod(unit, UNITS)
+            o, t = divmod(r, TILES)
             if t == 0:
-                grouped_tiles[j] = [
-                    work.tile(
-                        [P, ROUND_ROWS * PACK], BF16, name="grouped", tag="grouped%d" % o, align_bytes=64
-                    )
-                    for o in range(OPERANDS)
-                ]
-            for o in range(OPERANDS):
-                words = act_tiles[j][o][:, t, :].bitcast(F32)
-                grouped_words = grouped_tiles[j][o][:].bitcast(F32).rearrange("p (r u) -> p r u", u=2)
-                xt = psum.tile([P, 2, P], F32, name="xt", tag="xt", bufs=4)
-                for u in range(2):
-                    if (step, o) in sorted_tiles:
-                        source = sorted_tiles[(step, o)][:, u, :]
-                    else:
-                        source = words[:, u:WORDS:2]
-                    nc.tensor.transpose(xt[:, u, :], source, ident[:])
-                nc.scalar.copy(
-                    out=grouped_words[:, t * P : (t + 1) * P, :], in_=xt[:].rearrange("p u r -> p r u")
+                grouped_tiles[(j, o)] = work.tile(
+                    [P, ROUND_ROWS * PACK], BF16, name="grouped", tag="grouped%d" % o, align_bytes=64, bufs=2
                 )
+            words = act_tiles[(j, o)][:, t, :].bitcast(F32)
+            grouped_words = grouped_tiles[(j, o)][:].bitcast(F32).rearrange("p (r u) -> p r u", u=2)
+            xt = psum.tile([P, 2, P], F32, name="xt", tag="xt", bufs=4)
+            for u in range(2):
+                nc.tensor.transpose(xt[:, u, :], words[:, u:WORDS:2], ident[:])
+            nc.scalar.copy(out=grouped_words[:, t * P : (t + 1) * P, :], in_=xt[:].rearrange("p u r -> p r u"))
 
         def quantise(step):
-            j, part = divmod(step, STEPS)
-            if part == 0:
-                code_tiles[j] = [
-                    work.tile([P, ROUND_ROWS], U32, name="codes", tag="codes%d" % o, align_bytes=64)
-                    for o in range(OPERANDS)
-                ]
-                scale_tiles[j] = [
-                    work.tile([P, ROUND_ROWS], U8, name="scales", tag="scales%d" % o, align_bytes=64)
-                    for o in range(OPERANDS)
-                ]
-            first_row = part * STEP_TILES * P
-            rows = slice(first_row, first_row + STEP_TILES * P)
-            values = slice(first_row * PACK, (first_row + STEP_TILES * P) * PACK)
-            for o in range(OPERANDS):
-                nc.vector.quantize_mx(
-                    out=code_tiles[j][o][:, rows].bitcast(FP8X4),
-                    scales=scale_tiles[j][o][:, rows],
-                    in_=grouped_tiles[j][o][:, values],
-                )
+            j, o = divmod(step, STEPS)
+            if j < 0 or o >= OPERANDS or j >= ROUNDS:
+                return
+            codes = work.tile([P, ROUND_ROWS], U32, name="codes", tag="codes%d" % o, align_bytes=64)
+            scales = work.tile([P, ROUND_ROWS], U8, name="scales", tag="scales%d" % o, align_bytes=64)
+            nc.vector.quantize_mx(out=codes[:].bitcast(FP8X4), scales=scales[:], in_=grouped_tiles[(j, o)][:])
+            code_tiles[(j, o)] = codes
+            scale_tiles[(j, o)] = scales
 
         def gates(step):
             j, part = divmod(step, STEPS)
-            for s in range(part * STEP_TILES, (part + 1) * STEP_TILES):
+            for s in range(part, part + 1):
                 z = psum.tile([P, ROUND_ROWS], F32, name="z", tag="z")
                 for o in range(OPERANDS):
                     nc.tensor.matmul_mx(
                         out=z[:],
                         lhsT=w_bytes[o][:, s * P * PACK : (s + 1) * P * PACK].bitcast(FP8X4),
                         lhsT_scale=w_planes[:, o, s * P : (s + 1) * P],
-                        rhs=code_tiles[j][o][:].bitcast(FP8X4),
-                        rhs_scale=scale_tiles[j][o][:],
+                        rhs=code_tiles[(j, o)][:].bitcast(FP8X4),
+                        rhs_scale=scale_tiles[(j, o)][:],
                         start=(o == 0),
                         stop=(o == OPERANDS - 1),
                     )
-                att_t = work.tile([P, ROUND_ROWS], F32, name="att_t", tag="att_t", bufs=4 * STEP_TILES)
+                att_t = work.tile([P, ROUND_ROWS], F32, name="att_t", tag="att_t", bufs=4)
                 nc.scalar.activation(out=att_t[:], in_=z[:], func=ACT.Sigmoid, bias=bias_sb[:, s : s + 1])
                 att_t_tiles[(j, s)] = att_t
 
@@ -174,7 +141,7 @@ def tile_parentgru_pb_t_kernel(
             j, part = divmod(step, STEPS)
             if part == 0:
                 result_tiles[j] = work.tile([P, TILES, N], F32, name="result", tag="result", bufs=2)
-            for s in range(part * STEP_TILES, (part + 1) * STEP_TILES):
+            for s in range(part, part + 1):
                 features = slice(s * P, (s + 1) * P)
                 att = psum.tile([P, TILES, P], F32, name="att", tag="att")
                 for a in range(TILES):
@@ -186,7 +153,7 @@ def tile_parentgru_pb_t_kernel(
                     out=att_s[:],
                     in0=att[:],
                     scalar=-1.0,
-                    in1=act_tiles[j][STATE][:, :, features],
+                    in1=act_tiles[(j, STATE)][:, :, features],
                     op0=ALU.add,
                     op1=ALU.mult,
                 )
@@ -214,7 +181,8 @@ def tile_parentgru_pb_t_kernel(
         ident = consts.tile([P, P], F32, name="ident")
         make_identity(nc, ident[:])
 
-        load_activations(0)
+        load_activations(0, 2)
+        load_activation(1, 0)
         for o in range(OPERANDS):
             for r in range(4):
                 nc.sync.dma_start(
@@ -229,7 +197,10 @@ def tile_parentgru_pb_t_kernel(
                 in_=weight_words[o].rearrange("g p n t -> (g p) (n t)").bitcast(I32),
             )
             w_bytes.append(w_sb)
-        load_activations(1)
+        load_activation(1, 1)
+        load_activation(1, 2)
+        load_candidate(0)
+        load_activations(2)
 
         bias_rows_f32 = consts.tile([P, P], F32, name="bias_rows_f32")
         bias_sb = consts.tile([P, SLICES], F32, name="bias_sb")
@@ -238,20 +209,18 @@ def tile_parentgru_pb_t_kernel(
         nc.tensor.transpose(bias_t[:, 0:P], bias_rows_f32[:], ident[:])
         nc.vector.tensor_copy(out=bias_sb[:], in_=bias_t[:, 0:SLICES])
 
-        load_candidate(0)
-        load_activations(2)
         for step in range(-IN_LEAD, ALL_STEPS + OUT_LAG):
             j, part = divmod(step, STEPS)
             if part == 0 and 0 <= j < ROUNDS - 1:
                 load_candidate(j + 1)
             if part == 0 and 0 <= j < ROUNDS - LOAD_AHEAD:
                 load_activations(j + LOAD_AHEAD)
-            if step + IN_LEAD < ALL_STEPS:
-                transpose_in(step + IN_LEAD)
+            into = step + IN_LEAD
+            quantise(into - QUANTISE_LAG)
+            for unit in range(into * STEP_UNITS, (into + 1) * STEP_UNITS):
+                if unit < ROUNDS * UNITS:
+                    transpose_in(unit)
             if step - OUT_LAG >= 0:
                 blend(step - OUT_LAG)
-            if step + IN_LEAD < ALL_STEPS:
-                quantise(step + IN_LEAD)
             if 0 <= step < ALL_STEPS:
                 gates(step)
-            sort_words(step + IN_LEAD + SORT_AHEAD)

@@ -31,6 +31,7 @@ UNITS = OPERANDS * TILES
 STEP_UNITS = UNITS // STEPS
 IN_LEAD = 4
 QUANTISE_LAG = 2
+WARM_START, WARM_GATES = 4, 3
 OUT_LAG = 2
 LOAD_AHEAD = 3
 
@@ -180,6 +181,13 @@ def tile_parentgru_pb_t_kernel(
         nc.scalar.activation(out=warm_out[:], in_=warm_in[:], func=ACT.Sigmoid)
         ident = consts.tile([P, P], F32, name="ident")
         make_identity(nc, ident[:])
+        still = consts.tile([P, ROUND_ROWS], BF16, name="still")
+        nc.vector.memset(still[:], 0.0)
+
+        def keep_warm(count):
+            idle = psum.tile([P, ROUND_ROWS], F32, name="idle", tag="att")
+            for i in range(count):
+                nc.tensor.matmul(idle[:], lhsT=still[:, 0:P], rhs=still[:], start=True, stop=True)
 
         load_activations(0, 2)
         load_activation(1, 0)
@@ -202,6 +210,8 @@ def tile_parentgru_pb_t_kernel(
         load_candidate(0)
         load_activations(2)
 
+        keep_warm(WARM_START)
+
         bias_rows_f32 = consts.tile([P, P], F32, name="bias_rows_f32")
         bias_sb = consts.tile([P, SLICES], F32, name="bias_sb")
         nc.vector.tensor_copy(out=bias_rows_f32[:], in_=bias_rows[:])
@@ -222,5 +232,7 @@ def tile_parentgru_pb_t_kernel(
                     transpose_in(unit)
             if step - OUT_LAG >= 0:
                 blend(step - OUT_LAG)
+            if step == 0:
+                keep_warm(WARM_GATES)
             if 0 <= step < ALL_STEPS:
                 gates(step)

from contextlib import ExitStack

import concourse.mybir as mybir
from concourse.masks import make_identity

F32 = mybir.dt.float32
BF16 = mybir.dt.bfloat16
I32 = mybir.dt.int32
U32 = mybir.dt.uint32
U8 = mybir.dt.uint8
FP8X4 = mybir.dt.float8_e4m3fn_x4
ACT = mybir.ActivationFunctionType
ALU = mybir.AluOpType

P = 128
PACK = 4
B = 4096
K = 512
N = 512
OPERANDS = 3
STATE = 1
ROW_TILES = B // P
TILES = 4
ROUNDS = ROW_TILES // TILES
ROUND_ROWS = TILES * P
SLICES = N // P
WORDS = K // 2
STEPS = SLICES
ALL_STEPS = ROUNDS * STEPS
UNITS = OPERANDS * TILES
STEP_UNITS = UNITS // STEPS
IN_LEAD = 4
QUANTISE_LAG = 2
WARM_START, WARM_GATES = 4, 3
OUT_LAG = 2
LOAD_AHEAD = 3

FLOPS = 2 * B * K * N * OPERANDS


def tile_parentgru_pb_t_kernel(
    tc,
    inputs,
    state,
    parent_state,
    c,
    w_a_w_words,
    w_a_w_scales,
    w_a_b,
    u_a_w_words,
    u_a_w_scales,
    p_a_w_words,
    p_a_w_scales,
    out,
):
    nc = tc.nc
    activations = [inputs, state, parent_state]
    weight_words = [w_a_w_words, u_a_w_words, p_a_w_words]
    weight_scales = [w_a_w_scales, u_a_w_scales, p_a_w_scales]

    act_views = [x.rearrange("(p t) k -> p t k", t=ROW_TILES) for x in activations]
    c_view = c.rearrange("(p t) n -> p t n", t=ROW_TILES)
    out_view = out.rearrange("(p t) n -> p t n", t=ROW_TILES)

    with ExitStack() as ctx:
        consts = ctx.enter_context(tc.tile_pool(name="consts", bufs=1))
        stream = ctx.enter_context(tc.tile_pool(name="stream", bufs=3))
        work = ctx.enter_context(tc.tile_pool(name="work", bufs=3))
        psum = ctx.enter_context(tc.psum_pool(name="psum", bufs=2))
        ctx.enter_context(tc.manual_schedule())

        act_tiles = {}
        c_tiles = {}
        grouped_tiles = {}
        code_tiles = {}
        scale_tiles = {}
        att_t_tiles = {}
        result_tiles = {}

        def load_activation(j, o, parts=1):
            x_sb = stream.tile([P, TILES, K], BF16, name="x_sb", tag="x%d" % o, bufs=(6 if o == STATE else 4))
            size = TILES // parts
            for first in range(0, TILES, size):
                nc.sync.dma_start(
                    out=x_sb[:, first : first + size, :],
                    in_=act_views[o][:, j * TILES + first : j * TILES + first + size, :],
                )
            act_tiles[(j, o)] = x_sb

        def load_activations(j, parts=1):
            for o in range(OPERANDS):
                load_activation(j, o, parts)

        def load_candidate(j):
            c_sb = stream.tile([P, TILES, N], BF16, name="c_sb", tag="c")
            nc.sync.dma_start(out=c_sb[:], in_=c_view[:, j * TILES : (j + 1) * TILES, :])
            c_tiles[j] = c_sb

        def transpose_in(unit):
            j, r = divmod(unit, UNITS)
            o, t = divmod(r, TILES)
            if t == 0:
                grouped_tiles[(j, o)] = work.tile(
                    [P, ROUND_ROWS * PACK], BF16, name="grouped", tag="grouped%d" % o, align_bytes=64, bufs=2
                )
            words = act_tiles[(j, o)][:, t, :].bitcast(F32)
            grouped_words = grouped_tiles[(j, o)][:].bitcast(F32).rearrange("p (r u) -> p r u", u=2)
            xt = psum.tile([P, 2, P], F32, name="xt", tag="xt", bufs=4)
            for u in range(2):
                nc.tensor.transpose(xt[:, u, :], words[:, u:WORDS:2], ident[:])
            nc.scalar.copy(out=grouped_words[:, t * P : (t + 1) * P, :], in_=xt[:].rearrange("p u r -> p r u"))

        def quantise(step):
            j, o = divmod(step, STEPS)
            if j < 0 or o >= OPERANDS or j >= ROUNDS:
                return
            codes = work.tile([P, ROUND_ROWS], U32, name="codes", tag="codes%d" % o, align_bytes=64)
            scales = work.tile([P, ROUND_ROWS], U8, name="scales", tag="scales%d" % o, align_bytes=64)
            nc.vector.quantize_mx(out=codes[:].bitcast(FP8X4), scales=scales[:], in_=grouped_tiles[(j, o)][:])
            code_tiles[(j, o)] = codes
            scale_tiles[(j, o)] = scales

        def gates(step):
            j, part = divmod(step, STEPS)
            for s in range(part, part + 1):
                z = psum.tile([P, ROUND_ROWS], F32, name="z", tag="z")
                for o in range(OPERANDS):
                    nc.tensor.matmul_mx(
                        out=z[:],
                        lhsT=w_bytes[o][:, s * P * PACK : (s + 1) * P * PACK].bitcast(FP8X4),
                        lhsT_scale=w_planes[:, o, s * P : (s + 1) * P],
                        rhs=code_tiles[(j, o)][:].bitcast(FP8X4),
                        rhs_scale=scale_tiles[(j, o)][:],
                        start=(o == 0),
                        stop=(o == OPERANDS - 1),
                    )
                att_t = work.tile([P, ROUND_ROWS], F32, name="att_t", tag="att_t", bufs=4)
                nc.scalar.activation(out=att_t[:], in_=z[:], func=ACT.Sigmoid, bias=bias_sb[:, s : s + 1])
                att_t_tiles[(j, s)] = att_t

        def blend(step):
            j, part = divmod(step, STEPS)
            if part == 0:
                result_tiles[j] = work.tile([P, TILES, N], F32, name="result", tag="result", bufs=2)
            for s in range(part, part + 1):
                features = slice(s * P, (s + 1) * P)
                att = psum.tile([P, TILES, P], F32, name="att", tag="att")
                for a in range(TILES):
                    nc.tensor.transpose(att[:, a, :], att_t_tiles[(j, s)][:, a * P : (a + 1) * P], ident[:])
                att_c = work.tile([P, TILES, P], F32, name="att_c", tag="att_c")
                att_s = work.tile([P, TILES, P], F32, name="att_s", tag="att_s")
                nc.vector.tensor_tensor(out=att_c[:], in0=att[:], in1=c_tiles[j][:, :, features], op=ALU.mult)
                nc.vector.scalar_tensor_tensor(
                    out=att_s[:],
                    in0=att[:],
                    scalar=-1.0,
                    in1=act_tiles[(j, STATE)][:, :, features],
                    op0=ALU.add,
                    op1=ALU.mult,
                )
                last = j == ROUNDS - 1
                engine = nc.vector if last and s == SLICES - 1 else nc.gpsimd
                engine.tensor_tensor(
                    out=result_tiles[j][:, :, features], in0=att_c[:], in1=att_s[:], op=ALU.subtract
                )
                if last:
                    nc.sync.dma_start(
                        out=out_view[:, j * TILES : (j + 1) * TILES, features], in_=result_tiles[j][:, :, features]
                    )
            if part == STEPS - 1 and j < ROUNDS - 1:
                nc.sync.dma_start(out=out_view[:, j * TILES : (j + 1) * TILES, :], in_=result_tiles[j][:])

        w_planes = consts.tile([P, OPERANDS, N], U8, name="w_planes", align_bytes=64)
        nc.vector.memset(w_planes[:].bitcast(I32), 0)
        bias_rows = consts.tile([P, P], BF16, name="bias_rows")
        nc.vector.memset(bias_rows[:], 0.0)
        nc.sync.dma_start(out=bias_rows[0:SLICES, :], in_=w_a_b.rearrange("(s m) -> s m", m=P))
        warm_in = consts.tile([P, 1], F32, name="warm_in")
        warm_out = consts.tile([P, 1], F32, name="warm_out")
        nc.vector.memset(warm_in[:], 0.0)
        nc.scalar.activation(out=warm_out[:], in_=warm_in[:], func=ACT.Sigmoid)
        ident = consts.tile([P, P], F32, name="ident")
        make_identity(nc, ident[:])
        still = consts.tile([P, ROUND_ROWS], BF16, name="still")
        nc.vector.memset(still[:], 0.0)

        def keep_warm(count):
            idle = psum.tile([P, ROUND_ROWS], F32, name="idle", tag="att")
            for i in range(count):
                nc.tensor.matmul(idle[:], lhsT=still[:, 0:P], rhs=still[:], start=True, stop=True)

        load_activations(0, 2)
        load_activation(1, 0)
        for o in range(OPERANDS):
            for r in range(4):
                nc.sync.dma_start(
                    out=w_planes[r:P:32, o, :].bitcast(I32),
                    in_=weight_scales[o][0, r:16:4, :].bitcast(I32),
                )
        w_bytes = []
        for o in range(OPERANDS):
            w_sb = consts.tile([P, N * PACK], U8, name="w_sb%d" % o, align_bytes=64)
            nc.sync.dma_start(
                out=w_sb[:].bitcast(I32),
                in_=weight_words[o].rearrange("g p n t -> (g p) (n t)").bitcast(I32),
            )
            w_bytes.append(w_sb)
        load_activation(1, 1)
        load_activation(1, 2)
        load_candidate(0)
        load_activations(2)

        keep_warm(WARM_START)

        bias_rows_f32 = consts.tile([P, P], F32, name="bias_rows_f32")
        bias_sb = consts.tile([P, SLICES], F32, name="bias_sb")
        nc.vector.tensor_copy(out=bias_rows_f32[:], in_=bias_rows[:])
        bias_t = psum.tile([P, N], F32, name="bias_t", tag="att")
        nc.tensor.transpose(bias_t[:, 0:P], bias_rows_f32[:], ident[:])
        nc.vector.tensor_copy(out=bias_sb[:], in_=bias_t[:, 0:SLICES])

        for step in range(-IN_LEAD, ALL_STEPS + OUT_LAG):
            j, part = divmod(step, STEPS)
            if part == 0 and 0 <= j < ROUNDS - 1:
                load_candidate(j + 1)
            if part == 0 and 0 <= j < ROUNDS - LOAD_AHEAD:
                load_activations(j + LOAD_AHEAD)
            into = step + IN_LEAD
            quantise(into - QUANTISE_LAG)
            for unit in range(into * STEP_UNITS, (into + 1) * STEP_UNITS):
                if unit < ROUNDS * UNITS:
                    transpose_in(unit)
            if step - OUT_LAG >= 0:
                blend(step - OUT_LAG)
            if step == 0:
                keep_warm(WARM_GATES)
            if 0 <= step < ALL_STEPS:
                gates(step)
